import numpy as np
import ml_dtypes


def mxq(x, axis, fmt="e4m3"):
    dtype, down = {"e4m3": (ml_dtypes.float8_e4m3fn, 7), "e5m2": (ml_dtypes.float8_e5m2, 14)}[fmt]
    v = np.moveaxis(np.asarray(x, np.float32).astype(ml_dtypes.bfloat16).astype(np.float64), axis, -1)
    blocks = v.reshape(v.shape[:-1] + (-1, 32))
    amax = np.abs(blocks).max(-1, keepdims=True)
    byte = np.maximum(np.where(amax > 0, np.frexp(amax)[1] - 1 + 127, 0) - down, 1)
    scale = np.exp2(byte - 127.0)
    codes = (blocks / scale).astype(np.float32).astype(dtype).astype(np.float64)
    return np.moveaxis((codes * scale).reshape(v.shape), -1, axis)


WIDE = False


def mx_kscale(k):
    if not WIDE:
        return np.ones(k)
    levels = np.array([10, -10, 5, -5, 0])
    a = np.random.permutation(np.resize(levels, k // 512 * 4)).reshape(k // 512, 4)
    idx = np.arange(k)
    return np.exp2(a[idx // 512, idx % 128 // 32])


BF16 = ml_dtypes.bfloat16


def bf(x):
    return np.asarray(x, np.float32).astype(BF16)


def f64(x):
    return np.asarray(x).astype(np.float64)


B, N, F, U, S = 16, 512, 128, 128, 2
C = S * (F + U)


def sigmoid(v):
    return 1.0 / (1.0 + np.exp(-v))


def random_walk():
    a = np.random.uniform(size=(N, N))
    return a / a.sum(axis=1, keepdims=True) * np.sqrt(N)


def setup_inputs():
    s = mx_kscale(N)
    return {"inputs": bf((np.random.standard_normal((B, F, N)) * s).reshape(B, F * N)),
            "state": bf((np.random.standard_normal((B, U, N)) * s).reshape(B, U * N)),
            "support0": bf(random_walk() / s[None, :]),
            "support1": bf(random_walk() / s[None, :]),
            "r_kernel": bf(np.random.standard_normal((C, U)) / np.sqrt(C)),
            "u_kernel": bf(np.random.standard_normal((C, U)) / np.sqrt(C))}


def diffuse(xq, supq):
    return np.concatenate([(xq @ sq.T) for sq in supq], axis=1)


def reference(inputs, state, support0, support1, r_kernel, u_kernel):
    supq = (mxq(f64(support0), 1, "e4m3"), mxq(f64(support1), 1, "e4m3"))
    feats = f64(inputs).reshape(B, F, N)
    prev = f64(state).reshape(B, U, N)
    h = diffuse(mxq(feats, 2, "e4m3"), supq).transpose(0, 2, 1)
    st = diffuse(mxq(prev, 2, "e4m3"), supq).transpose(0, 2, 1)
    hsq = mxq(np.concatenate([h, st], axis=-1), 2, "e4m3")
    r = sigmoid(hsq @ mxq(f64(r_kernel), 0, "e4m3"))
    u = sigmoid(hsq @ mxq(f64(u_kernel), 0, "e4m3"))
    return r, u, h

@@ -1,0 +1,247 @@
+from contextlib import ExitStack
+
+import concourse.mybir as mybir
+from concourse.masks import make_identity
+
+F32 = mybir.dt.float32
+BF16 = mybir.dt.bfloat16
+U32 = mybir.dt.uint32
+U8 = mybir.dt.uint8
+FP8X4 = mybir.dt.float8_e4m3fn_x4
+SIGMOID = mybir.ActivationFunctionType.Sigmoid
+
+P = 128
+PACK = 4
+BANK = 512
+PSUM_BANKS = 8
+
+BATCH = 16
+NODES = 512
+CHANNELS = 128
+SIGNALS = 2
+SUPPORTS = 2
+GATES = 2
+NODE_TILES = NODES // P
+ROW_WORDS = NODES // 2
+HALVES = ROW_WORDS // P
+GROUP = BANK // CHANNELS
+GROUPS = BATCH // GROUP
+
+FLOPS = 2 * BATCH * NODES * NODES * SUPPORTS * SIGNALS * CHANNELS + 2 * BATCH * NODES * (PACK * CHANNELS) * GATES * CHANNELS
+
+
+def columns(first, count):
+    return slice(first, first + count)
+
+
+def tile_gcrnncell_pa_t_kernel(tc, inputs, state, support0, support1, r_kernel, u_kernel, out_0, out_1, out_2):
+    nc = tc.nc
+    with ExitStack() as stack:
+        stack.enter_context(tc.manual_schedule())
+        const = stack.enter_context(tc.tile_pool(name="const", bufs=1))
+        rows_pool = stack.enter_context(tc.tile_pool(name="rows", bufs=GROUPS))
+        group_pool = stack.enter_context(tc.tile_pool(name="group", bufs=2))
+        batch_pool = stack.enter_context(tc.tile_pool(name="batch", bufs=3))
+        h_pool = stack.enter_context(tc.tile_pool(name="h", bufs=3))
+        gate_pool = stack.enter_context(tc.tile_pool(name="gate", bufs=8))
+        psum = stack.enter_context(tc.psum_pool(name="psum", bufs=PSUM_BANKS))
+
+        sup_rows = const.tile([P, SUPPORTS * NODES * NODE_TILES], BF16)
+        for i, support in enumerate((support0, support1)):
+            nc.sync.dma_start(
+                out=sup_rows[:, columns(i * NODE_TILES * NODES, NODE_TILES * NODES)],
+                in_=support.rearrange("(p t) n -> p (t n)", t=NODE_TILES),
+            )
+
+        def load_group(g):
+            x_rows = rows_pool.tile([P, SIGNALS * GROUP * NODES], BF16, tag="x_rows")
+            by_signal = x_rows[:].rearrange("c (x b n) -> c x b n", x=SIGNALS, b=GROUP)
+            for x, signal in enumerate((inputs, state)):
+                nc.sync.dma_start(
+                    out=by_signal[:, x],
+                    in_=signal[columns(g * GROUP, GROUP), :].rearrange("b (c n) -> c b n", n=NODES),
+                )
+            return x_rows
+
+        x_rows_of = [load_group(0)]
+
+        gate_rows = const.tile([P, GATES * PACK * CHANNELS], BF16)
+        gate_rows_by_gate = gate_rows[:].rearrange("c (g j u) -> c g j u", g=GATES, j=PACK)
+        for gate, kernel in enumerate((r_kernel, u_kernel)):
+            nc.sync.dma_start(out=gate_rows_by_gate[:, gate], in_=kernel.rearrange("(j c) u -> c j u", c=P))
+
+        for g in range(1, GROUPS):
+            x_rows_of.append(load_group(g))
+
+        identity = const.tile([P, P], F32)
+        make_identity(nc, identity[:])
+        table_warmer = const.tile([P, 1], F32)
+        nc.scalar.activation(out=table_warmer[:], in_=identity[:, 0:1], func=SIGMOID)
+
+        def empty_bank(index, out, in_):
+            if index % 2 == 0:
+                nc.vector.tensor_copy(out=out, in_=in_)
+            else:
+                nc.scalar.copy(out=out, in_=in_)
+
+        def flip_two_blocks(index, row_words, quad_words):
+            bank = psum.tile([P, BANK], F32, tag="bank")
+            flipped = bank[:].rearrange("w (k u r) -> w k u r", k=2, u=HALVES)
+            for k in range(2):
+                for u in range(HALVES):
+                    nc.tensor.transpose(flipped[:, k, u, :], row_words[:, k, columns(u * P, P)], identity[:])
+            empty_bank(index, quad_words, flipped.rearrange("w k u r -> w k r u"))
+
+        def quantise(quads, operand, first_word, words):
+            codes, scales = operand
+            nc.vector.quantize_mx(
+                out=codes[:, columns(first_word, words)].bitcast(FP8X4),
+                scales=scales[:, columns(first_word, words)],
+                in_=quads[:, columns(PACK * first_word, PACK * words)],
+            )
+
+        def multiply(out, stationary, stationary_columns, moving, moving_columns):
+            nc.tensor.matmul_mx(
+                out=out,
+                lhsT=stationary[0][:, stationary_columns].bitcast(FP8X4),
+                lhsT_scale=stationary[1][:, stationary_columns],
+                rhs=moving[0][:, moving_columns].bitcast(FP8X4),
+                rhs_scale=moving[1][:, moving_columns],
+                start=True,
+                stop=True,
+            )
+
+        sup_words = NODE_TILES * SUPPORTS * P
+        sup_quads = const.tile([P, sup_words * PACK], BF16, align_bytes=64)
+        sup_codes = const.tile([P, sup_words], U32, align_bytes=64)
+        sup_scales = const.tile([P, sup_words], U8, align_bytes=64)
+        sup_mx = (sup_codes, sup_scales)
+        sup_row_words = sup_rows[:].bitcast(F32).rearrange("p (i t w) -> p i t w", i=SUPPORTS, t=NODE_TILES)
+        sup_quad_words = sup_quads[:].bitcast(F32).rearrange(
+            "w (t i p u) -> w i t p u", t=NODE_TILES, i=SUPPORTS, u=HALVES
+        )
+        for i in range(SUPPORTS):
+            for pair in range(NODE_TILES // 2):
+                tiles = columns(2 * pair, 2)
+                flip_two_blocks(pair, sup_row_words[:, i, tiles, :], sup_quad_words[:, i, tiles, :, :])
+        for half in range(2):
+            quantise(sup_quads, sup_mx, half * sup_words // 2, sup_words // 2)
+
+        signal_words = GROUP * CHANNELS
+
+        def flip_group(g):
+            x_quads = group_pool.tile([P, SIGNALS * signal_words * PACK], BF16, tag="x_quads", align_bytes=64)
+            x_codes = group_pool.tile([P, SIGNALS * signal_words], U32, tag="x_codes", align_bytes=64)
+            x_scales = group_pool.tile([P, SIGNALS * signal_words], U8, tag="x_scales", align_bytes=64)
+            row_words = x_rows_of[g][:].bitcast(F32).rearrange("c (k w) -> c k w", w=ROW_WORDS)
+            quad_words = x_quads[:].bitcast(F32).rearrange("w (k c u) -> w k c u", c=CHANNELS, u=HALVES)
+            for pair in range(SIGNALS * GROUP // 2):
+                blocks = columns(2 * pair, 2)
+                flip_two_blocks(pair, row_words[:, blocks, :], quad_words[:, blocks, :, :])
+            return x_quads, (x_codes, x_scales)
+
+        def quantise_group(x_quads, x_mx):
+            for x in range(SIGNALS):
+                quantise(x_quads, x_mx, x * signal_words, signal_words)
+
+        def diffuse_for_gates(b, x_mx):
+            hs_quads = batch_pool.tile([P, NODES * PACK], BF16, tag="hs_quads", align_bytes=64)
+            for t in range(NODE_TILES):
+                bank = psum.tile([P, BANK], F32, tag="bank")
+                for x in range(SIGNALS):
+                    multiply(
+                        bank[:, columns(x * SUPPORTS * P, SUPPORTS * P)],
+                        x_mx,
+                        columns((x * GROUP + b % GROUP) * CHANNELS, CHANNELS),
+                        sup_mx,
+                        columns(t * SUPPORTS * P, SUPPORTS * P),
+                    )
+                empty_bank(
+                    t,
+                    hs_quads[:, columns(t * P * PACK, P * PACK)].rearrange("c (p j) -> c p j", j=PACK),
+                    bank[:].rearrange("c (j p) -> c p j", j=PACK),
+                )
+            return hs_quads
+
+        def quantise_hs(hs_quads):
+            hs_codes = batch_pool.tile([P, NODES], U32, tag="hs_codes", align_bytes=64)
+            hs_scales = batch_pool.tile([P, NODES], U8, tag="hs_scales", align_bytes=64)
+            quantise(hs_quads, (hs_codes, hs_scales), 0, NODES)
+            return hs_codes, hs_scales
+
+        def diffuse_for_output(i, x_mx, h_rows):
+            by_tile = h_rows[:].rearrange("p (b t i c) -> p t i b c", b=GROUP, t=NODE_TILES, i=SUPPORTS)
+            for t in range(NODE_TILES):
+                bank = psum.tile([P, BANK], F32, tag="bank")
+                multiply(bank[:], sup_mx, columns((t * SUPPORTS + i) * P, P), x_mx, columns(0, signal_words))
+                empty_bank(t, by_tile[:, t, i], bank[:].rearrange("p (b c) -> p b c", b=GROUP))
+
+        def store_h(g, h_rows):
+            nc.sync.dma_start(
+                out=out_2[columns(g * GROUP, GROUP)].rearrange("b (p t) k -> p b (t k)", t=NODE_TILES),
+                in_=h_rows[:].rearrange("p (b r) -> p b r", b=GROUP),
+            )
+
+        gate_words = GATES * CHANNELS
+        gate_quads = const.tile([P, gate_words * PACK], BF16, align_bytes=64)
+        gate_codes = const.tile([P, gate_words], U32, align_bytes=64)
+        gate_scales = const.tile([P, gate_words], U8, align_bytes=64)
+        gate_mx = (gate_codes, gate_scales)
+
+        def gates(b, hs_mx):
+            gate_values = gate_pool.tile([P, GATES * NODE_TILES * CHANNELS], F32, tag="gate_values")
+            by_tile = gate_values[:].rearrange("p (g t u) -> p t g u", g=GATES, t=NODE_TILES)
+            for pair in range(NODE_TILES // 2):
+                bank = psum.tile([P, BANK], F32, tag="bank")
+                for k in range(2):
+                    multiply(
+                        bank[:, columns(k * gate_words, gate_words)],
+                        hs_mx,
+                        columns((2 * pair + k) * P, P),
+                        gate_mx,
+                        columns(0, gate_words),
+                    )
+                nc.scalar.activation(
+                    out=by_tile[:, columns(2 * pair, 2)],
+                    in_=bank[:].rearrange("p (t g u) -> p t g u", t=2, g=GATES),
+                    func=SIGMOID,
+                )
+            for gate, result in enumerate((out_0, out_1)):
+                nc.sync.dma_start(
+                    out=result[b].rearrange("(p t) u -> p (t u)", t=NODE_TILES),
+                    in_=gate_values[:, columns(gate * NODE_TILES * CHANNELS, NODE_TILES * CHANNELS)],
+                )
+
+        x_quads, x_mx = flip_group(0)
+        quantise_group(x_quads, x_mx)
+        nc.vector.tensor_copy(
+            out=gate_quads[:].rearrange("c (g u j) -> c g u j", g=GATES, j=PACK),
+            in_=gate_rows_by_gate.rearrange("c g j u -> c g u j"),
+        )
+        h_rows = h_pool.tile([P, GROUP * NODE_TILES * SUPPORTS * CHANNELS], F32, tag="h_rows")
+        diffuse_for_output(0, x_mx, h_rows)
+        quantise(gate_quads, gate_mx, 0, gate_words)
+        diffuse_for_output(1, x_mx, h_rows)
+        store_h(0, h_rows)
+
+        for b in range(BATCH):
+            g, turn = divmod(b, GROUP)
+            prepare = g + 1 < GROUPS
+            hs_quads = diffuse_for_gates(b, x_mx)
+            if prepare and turn == 0:
+                next_quads, next_mx = flip_group(g + 1)
+            if prepare and turn == 1:
+                h_rows = h_pool.tile([P, GROUP * NODE_TILES * SUPPORTS * CHANNELS], F32, tag="h_rows")
+                diffuse_for_output(0, next_mx, h_rows)
+            if prepare and turn == 2:
+                diffuse_for_output(1, next_mx, h_rows)
+                store_h(g + 1, h_rows)
+            hs_mx = quantise_hs(hs_quads)
+            if prepare and turn == 0:
+                quantise_group(next_quads, next_mx)
+            if b > 0:
+                gates(b - 1, earlier_hs_mx)
+            earlier_hs_mx = hs_mx
+            if prepare and turn == GROUP - 1:
+                x_mx = next_mx
+        gates(BATCH - 1, earlier_hs_mx)

@@ -228,16 +228,16 @@ def tile_gcrnncell_pa_t_kernel(tc, inputs, state, support0, support1, r_kernel, 
             g, turn = divmod(b, GROUP)
             prepare = g + 1 < GROUPS
             hs_quads = diffuse_for_gates(b, x_mx)
-            if prepare and turn == 0:
-                next_quads, next_mx = flip_group(g + 1)
             if prepare and turn == 1:
+                next_quads, next_mx = flip_group(g + 1)
+            if prepare and turn == 2:
                 h_rows = h_pool.tile([P, GROUP * NODE_TILES * SUPPORTS * CHANNELS], F32, tag="h_rows")
                 diffuse_for_output(0, next_mx, h_rows)
-            if prepare and turn == 2:
+            if prepare and turn == 3:
                 diffuse_for_output(1, next_mx, h_rows)
                 store_h(g + 1, h_rows)
             hs_mx = quantise_hs(hs_quads)
-            if prepare and turn == 0:
+            if prepare and turn == 1:
                 quantise_group(next_quads, next_mx)
             if b > 0:
                 gates(b - 1, earlier_hs_mx)

@@ -24,7 +24,7 @@ GATES = 2
 NODE_TILES = NODES // P
 ROW_WORDS = NODES // 2
 HALVES = ROW_WORDS // P
-GROUP = BANK // CHANNELS
+GROUP = 2
 GROUPS = BATCH // GROUP
 
 FLOPS = 2 * BATCH * NODES * NODES * SUPPORTS * SIGNALS * CHANNELS + 2 * BATCH * NODES * (PACK * CHANNELS) * GATES * CHANNELS
@@ -40,18 +40,23 @@ def tile_gcrnncell_pa_t_kernel(tc, inputs, state, support0, support1, r_kernel, 
         stack.enter_context(tc.manual_schedule())
         const = stack.enter_context(tc.tile_pool(name="const", bufs=1))
         rows_pool = stack.enter_context(tc.tile_pool(name="rows", bufs=GROUPS))
-        group_pool = stack.enter_context(tc.tile_pool(name="group", bufs=2))
+        group_pool = stack.enter_context(tc.tile_pool(name="group", bufs=3))
         batch_pool = stack.enter_context(tc.tile_pool(name="batch", bufs=3))
-        h_pool = stack.enter_context(tc.tile_pool(name="h", bufs=3))
+        h_pool = stack.enter_context(tc.tile_pool(name="h", bufs=4))
         gate_pool = stack.enter_context(tc.tile_pool(name="gate", bufs=8))
         psum = stack.enter_context(tc.psum_pool(name="psum", bufs=PSUM_BANKS))
 
         sup_rows = const.tile([P, SUPPORTS * NODES * NODE_TILES], BF16)
-        for i, support in enumerate((support0, support1)):
-            nc.sync.dma_start(
-                out=sup_rows[:, columns(i * NODE_TILES * NODES, NODE_TILES * NODES)],
-                in_=support.rearrange("(p t) n -> p (t n)", t=NODE_TILES),
-            )
+        sup_rows_by_tile = sup_rows[:].rearrange("p (i t n) -> p i t n", i=SUPPORTS, t=NODE_TILES)
+        supports = (support0, support1)
+
+        def load_supports(pair):
+            for i in range(SUPPORTS):
+                tiles = columns(2 * pair, 2)
+                nc.sync.dma_start(
+                    out=sup_rows_by_tile[:, i, tiles, :],
+                    in_=supports[i].rearrange("(p t) n -> p t n", t=NODE_TILES)[:, tiles, :],
+                )
 
         def load_group(g):
             x_rows = rows_pool.tile([P, SIGNALS * GROUP * NODES], BF16, tag="x_rows")
@@ -63,14 +68,18 @@ def tile_gcrnncell_pa_t_kernel(tc, inputs, state, support0, support1, r_kernel, 
                 )
             return x_rows
 
-        x_rows_of = [load_group(0)]
+        x_rows_of = []
+        load_supports(0)
+        x_rows_of.append(load_group(0))
+        load_supports(1)
+        x_rows_of.append(load_group(1))
 
         gate_rows = const.tile([P, GATES * PACK * CHANNELS], BF16)
         gate_rows_by_gate = gate_rows[:].rearrange("c (g j u) -> c g j u", g=GATES, j=PACK)
         for gate, kernel in enumerate((r_kernel, u_kernel)):
             nc.sync.dma_start(out=gate_rows_by_gate[:, gate], in_=kernel.rearrange("(j c) u -> c j u", c=P))
 
-        for g in range(1, GROUPS):
+        for g in range(2, GROUPS):
             x_rows_of.append(load_group(g))
 
         identity = const.tile([P, P], F32)
@@ -78,19 +87,19 @@ def tile_gcrnncell_pa_t_kernel(tc, inputs, state, support0, support1, r_kernel, 
         table_warmer = const.tile([P, 1], F32)
         nc.scalar.activation(out=table_warmer[:], in_=identity[:, 0:1], func=SIGMOID)
 
-        def empty_bank(index, out, in_):
-            if index % 2 == 0:
+        def empty_bank(engine, out, in_):
+            if engine == "V":
                 nc.vector.tensor_copy(out=out, in_=in_)
             else:
                 nc.scalar.copy(out=out, in_=in_)
 
-        def flip_two_blocks(index, row_words, quad_words):
+        def flip_two_blocks(engine, row_words, quad_words):
             bank = psum.tile([P, BANK], F32, tag="bank")
             flipped = bank[:].rearrange("w (k u r) -> w k u r", k=2, u=HALVES)
             for k in range(2):
                 for u in range(HALVES):
                     nc.tensor.transpose(flipped[:, k, u, :], row_words[:, k, columns(u * P, P)], identity[:])
-            empty_bank(index, quad_words, flipped.rearrange("w k u r -> w k r u"))
+            empty_bank(engine, quad_words, flipped.rearrange("w k u r -> w k r u"))
 
         def quantise(quads, operand, first_word, words):
             codes, scales = operand
@@ -120,33 +129,40 @@ def tile_gcrnncell_pa_t_kernel(tc, inputs, state, support0, support1, r_kernel, 
         sup_quad_words = sup_quads[:].bitcast(F32).rearrange(
             "w (t i p u) -> w i t p u", t=NODE_TILES, i=SUPPORTS, u=HALVES
         )
-        for i in range(SUPPORTS):
-            for pair in range(NODE_TILES // 2):
-                tiles = columns(2 * pair, 2)
-                flip_two_blocks(pair, sup_row_words[:, i, tiles, :], sup_quad_words[:, i, tiles, :, :])
-        for half in range(2):
-            quantise(sup_quads, sup_mx, half * sup_words // 2, sup_words // 2)
+
+        def flip_supports(pair, engines):
+            tiles = columns(2 * pair, 2)
+            for i in range(SUPPORTS):
+                flip_two_blocks(engines[i], sup_row_words[:, i, tiles, :], sup_quad_words[:, i, tiles, :, :])
+
+        def quantise_supports(pair):
+            quantise(sup_quads, sup_mx, pair * sup_words // 2, sup_words // 2)
 
         signal_words = GROUP * CHANNELS
 
-        def flip_group(g):
+        def start_group():
             x_quads = group_pool.tile([P, SIGNALS * signal_words * PACK], BF16, tag="x_quads", align_bytes=64)
             x_codes = group_pool.tile([P, SIGNALS * signal_words], U32, tag="x_codes", align_bytes=64)
             x_scales = group_pool.tile([P, SIGNALS * signal_words], U8, tag="x_scales", align_bytes=64)
-            row_words = x_rows_of[g][:].bitcast(F32).rearrange("c (k w) -> c k w", w=ROW_WORDS)
-            quad_words = x_quads[:].bitcast(F32).rearrange("w (k c u) -> w k c u", c=CHANNELS, u=HALVES)
-            for pair in range(SIGNALS * GROUP // 2):
-                blocks = columns(2 * pair, 2)
-                flip_two_blocks(pair, row_words[:, blocks, :], quad_words[:, blocks, :, :])
             return x_quads, (x_codes, x_scales)
 
-        def quantise_group(x_quads, x_mx):
-            for x in range(SIGNALS):
-                quantise(x_quads, x_mx, x * signal_words, signal_words)
+        def flip_signal(g, x, x_quads, engine):
+            row_words = x_rows_of[g][:].bitcast(F32).rearrange("c (k w) -> c k w", w=ROW_WORDS)
+            quad_words = x_quads[:].bitcast(F32).rearrange("w (k c u) -> w k c u", c=CHANNELS, u=HALVES)
+            blocks = columns(2 * x, 2)
+            flip_two_blocks(engine, row_words[:, blocks, :], quad_words[:, blocks, :, :])
 
-        def diffuse_for_gates(b, x_mx):
+        def quantise_signal(x, x_quads, x_mx):
+            quantise(x_quads, x_mx, x * signal_words, signal_words)
+
+        def start_hs():
             hs_quads = batch_pool.tile([P, NODES * PACK], BF16, tag="hs_quads", align_bytes=64)
-            for t in range(NODE_TILES):
+            hs_codes = batch_pool.tile([P, NODES], U32, tag="hs_codes", align_bytes=64)
+            hs_scales = batch_pool.tile([P, NODES], U8, tag="hs_scales", align_bytes=64)
+            return hs_quads, (hs_codes, hs_scales)
+
+        def diffuse_for_gates(b, x_mx, hs_quads, tiles, engines):
+            for t, engine in zip(tiles, engines):
                 bank = psum.tile([P, BANK], F32, tag="bank")
                 for x in range(SIGNALS):
                     multiply(
@@ -157,24 +173,31 @@ def tile_gcrnncell_pa_t_kernel(tc, inputs, state, support0, support1, r_kernel, 
                         columns(t * SUPPORTS * P, SUPPORTS * P),
                     )
                 empty_bank(
-                    t,
+                    engine,
                     hs_quads[:, columns(t * P * PACK, P * PACK)].rearrange("c (p j) -> c p j", j=PACK),
                     bank[:].rearrange("c (j p) -> c p j", j=PACK),
                 )
-            return hs_quads
 
-        def quantise_hs(hs_quads):
-            hs_codes = batch_pool.tile([P, NODES], U32, tag="hs_codes", align_bytes=64)
-            hs_scales = batch_pool.tile([P, NODES], U8, tag="hs_scales", align_bytes=64)
-            quantise(hs_quads, (hs_codes, hs_scales), 0, NODES)
-            return hs_codes, hs_scales
+        def quantise_hs(hs_quads, hs_mx, tiles):
+            quantise(hs_quads, hs_mx, tiles[0] * P, len(tiles) * P)
 
-        def diffuse_for_output(i, x_mx, h_rows):
+        def start_h():
+            h_rows = h_pool.tile([P, GROUP * NODE_TILES * SUPPORTS * CHANNELS], F32, tag="h_rows")
+            return h_rows
+
+        def diffuse_for_output(g, x_mx, h_rows, tiles, engines):
             by_tile = h_rows[:].rearrange("p (b t i c) -> p t i b c", b=GROUP, t=NODE_TILES, i=SUPPORTS)
-            for t in range(NODE_TILES):
+            for t, engine in zip(tiles, engines):
                 bank = psum.tile([P, BANK], F32, tag="bank")
-                multiply(bank[:], sup_mx, columns((t * SUPPORTS + i) * P, P), x_mx, columns(0, signal_words))
-                empty_bank(t, by_tile[:, t, i], bank[:].rearrange("p (b c) -> p b c", b=GROUP))
+                for i in range(SUPPORTS):
+                    multiply(
+                        bank[:, columns(i * signal_words, signal_words)],
+                        sup_mx,
+                        columns((t * SUPPORTS + i) * P, P),
+                        x_mx,
+                        columns(0, signal_words),
+                    )
+                empty_bank(engine, by_tile[:, t], bank[:].rearrange("p (i b c) -> p i b c", i=SUPPORTS, b=GROUP))
 
         def store_h(g, h_rows):
             nc.sync.dma_start(
@@ -188,10 +211,13 @@ def tile_gcrnncell_pa_t_kernel(tc, inputs, state, support0, support1, r_kernel, 
         gate_scales = const.tile([P, gate_words], U8, align_bytes=64)
         gate_mx = (gate_codes, gate_scales)
 
-        def gates(b, hs_mx):
+        def start_gates():
             gate_values = gate_pool.tile([P, GATES * NODE_TILES * CHANNELS], F32, tag="gate_values")
+            return gate_values
+
+        def gates(hs_mx, gate_values, pairs):
             by_tile = gate_values[:].rearrange("p (g t u) -> p t g u", g=GATES, t=NODE_TILES)
-            for pair in range(NODE_TILES // 2):
+            for pair in pairs:
                 bank = psum.tile([P, BANK], F32, tag="bank")
                 for k in range(2):
                     multiply(
@@ -206,42 +232,80 @@ def tile_gcrnncell_pa_t_kernel(tc, inputs, state, support0, support1, r_kernel, 
                     in_=bank[:].rearrange("p (t g u) -> p t g u", t=2, g=GATES),
                     func=SIGMOID,
                 )
+
+        def store_gates(b, gate_values, first_tile, tiles):
             for gate, result in enumerate((out_0, out_1)):
                 nc.sync.dma_start(
-                    out=result[b].rearrange("(p t) u -> p (t u)", t=NODE_TILES),
-                    in_=gate_values[:, columns(gate * NODE_TILES * CHANNELS, NODE_TILES * CHANNELS)],
+                    out=result[b].rearrange("(p t) u -> p (t u)", t=NODE_TILES)[:, columns(first_tile * CHANNELS, tiles * CHANNELS)],
+                    in_=gate_values[:, columns((gate * NODE_TILES + first_tile) * CHANNELS, tiles * CHANNELS)],
                 )
 
-        x_quads, x_mx = flip_group(0)
-        quantise_group(x_quads, x_mx)
-        nc.vector.tensor_copy(
-            out=gate_quads[:].rearrange("c (g u j) -> c g u j", g=GATES, j=PACK),
-            in_=gate_rows_by_gate.rearrange("c g j u -> c g u j"),
-        )
-        h_rows = h_pool.tile([P, GROUP * NODE_TILES * SUPPORTS * CHANNELS], F32, tag="h_rows")
-        diffuse_for_output(0, x_mx, h_rows)
-        quantise(gate_quads, gate_mx, 0, gate_words)
-        diffuse_for_output(1, x_mx, h_rows)
-        store_h(0, h_rows)
+        def all_gates(b, hs_mx):
+            gate_values = start_gates()
+            gates(hs_mx, gate_values, (0, 1))
+            store_gates(b, gate_values, 0, NODE_TILES)
 
+        flip_supports(0, "SS")
+        quantise_supports(0)
+        x_quads, x_mx = start_group()
+        flip_signal(0, 0, x_quads, "S")
+        quantise_signal(0, x_quads, x_mx)
+        flip_signal(0, 1, x_quads, "S")
+        quantise_signal(1, x_quads, x_mx)
+        flip_supports(1, "SV")
+        h_rows = start_h()
+        diffuse_for_output(0, x_mx, h_rows, (0, 1), "SS")
+        quantise_supports(1)
+        first_halves = []
+        for b in range(GROUP):
+            hs_quads, hs_mx = start_hs()
+            diffuse_for_gates(b, x_mx, hs_quads, (0, 1), "SV")
+            first_halves.append((hs_quads, hs_mx))
+        diffuse_for_output(0, x_mx, h_rows, (2, 3), "SV")
+        store_h(0, h_rows)
+        waiting = None
         for b in range(BATCH):
             g, turn = divmod(b, GROUP)
-            prepare = g + 1 < GROUPS
-            hs_quads = diffuse_for_gates(b, x_mx)
-            if prepare and turn == 1:
-                next_quads, next_mx = flip_group(g + 1)
-            if prepare and turn == 2:
-                h_rows = h_pool.tile([P, GROUP * NODE_TILES * SUPPORTS * CHANNELS], F32, tag="h_rows")
-                diffuse_for_output(0, next_mx, h_rows)
-            if prepare and turn == 3:
-                diffuse_for_output(1, next_mx, h_rows)
-                store_h(g + 1, h_rows)
-            hs_mx = quantise_hs(hs_quads)
-            if prepare and turn == 1:
-                quantise_group(next_quads, next_mx)
-            if b > 0:
-                gates(b - 1, earlier_hs_mx)
-            earlier_hs_mx = hs_mx
-            if prepare and turn == GROUP - 1:
+            last = g + 1 == GROUPS
+            if b < GROUP:
+                hs_quads, hs_mx = first_halves[b]
+                diffuse_for_gates(b, x_mx, hs_quads, (2, 3), "SV")
+            else:
+                hs_quads, hs_mx = start_hs()
+                if b == BATCH - 1:
+                    diffuse_for_gates(b, x_mx, hs_quads, (0, 1), "VS")
+                    quantise_hs(hs_quads, hs_mx, (0, 1))
+                    diffuse_for_gates(b, x_mx, hs_quads, (2, 3), "VV")
+                    quantise_hs(hs_quads, hs_mx, (2, 3))
+                else:
+                    diffuse_for_gates(b, x_mx, hs_quads, (0, 1, 2, 3), "SVSV")
+            if not last:
+                if turn == 0:
+                    next_quads, next_mx = start_group()
+                    flip_signal(g + 1, 0, next_quads, "S" if g == 0 else "V")
+                    flip_signal(g + 1, 1, next_quads, "SVS"[0 if g == 0 else 1 + g % 2])
+                else:
+                    h_rows = start_h()
+                    diffuse_for_output(g + 1, next_mx, h_rows, (0, 1, 2, 3), "SVSV")
+                    store_h(g + 1, h_rows)
+            if b < BATCH - 1:
+                quantise_hs(hs_quads, hs_mx, (0, 1, 2, 3))
+            if turn == 0 and not last:
+                quantise_signal(0, next_quads, next_mx)
+                quantise_signal(1, next_quads, next_mx)
+            if b == 0:
+                nc.vector.tensor_copy(
+                    out=gate_quads[:].rearrange("c (g u j) -> c g u j", g=GATES, j=PACK),
+                    in_=gate_rows_by_gate.rearrange("c g j u -> c g u j"),
+                )
+            if b == 1:
+                quantise(gate_quads, gate_mx, 0, gate_words)
+            if waiting:
+                all_gates(*waiting)
+            waiting = (b, hs_mx)
+            if turn == 1 and not last:
                 x_mx = next_mx
-        gates(BATCH - 1, earlier_hs_mx)
+        gate_values = start_gates()
+        for pair in range(2):
+            gates(hs_mx, gate_values, (pair,))
+            store_gates(BATCH - 1, gate_values, 2 * pair, 2)

@@ -275,7 +275,7 @@ def tile_gcrnncell_pa_t_kernel(tc, inputs, state, support0, support1, r_kernel, 
                 if b == BATCH - 1:
                     diffuse_for_gates(b, x_mx, hs_quads, (0, 1), "VS")
                     quantise_hs(hs_quads, hs_mx, (0, 1))
-                    diffuse_for_gates(b, x_mx, hs_quads, (2, 3), "VV")
+                    diffuse_for_gates(b, x_mx, hs_quads, (2, 3), "VS")
                     quantise_hs(hs_quads, hs_mx, (2, 3))
                 else:
                     diffuse_for_gates(b, x_mx, hs_quads, (0, 1, 2, 3), "SVSV")
@@ -285,6 +285,8 @@ def tile_gcrnncell_pa_t_kernel(tc, inputs, state, support0, support1, r_kernel, 
                     flip_signal(g + 1, 0, next_quads, "S" if g == 0 else "V")
                     flip_signal(g + 1, 1, next_quads, "SVS"[0 if g == 0 else 1 + g % 2])
                 else:
+                    if g == 0:
+                        quantise(gate_quads, gate_mx, 0, gate_words)
                     h_rows = start_h()
                     diffuse_for_output(g + 1, next_mx, h_rows, (0, 1, 2, 3), "SVSV")
                     store_h(g + 1, h_rows)
@@ -298,8 +300,6 @@ def tile_gcrnncell_pa_t_kernel(tc, inputs, state, support0, support1, r_kernel, 
                     out=gate_quads[:].rearrange("c (g u j) -> c g u j", g=GATES, j=PACK),
                     in_=gate_rows_by_gate.rearrange("c g j u -> c g u j"),
                 )
-            if b == 1:
-                quantise(gate_quads, gate_mx, 0, gate_words)
             if waiting:
                 all_gates(*waiting)
             waiting = (b, hs_mx)

@@ -60,11 +60,11 @@ def tile_gcrnncell_pa_t_kernel(tc, inputs, state, support0, support1, r_kernel, 
 
         def load_group(g):
             x_rows = rows_pool.tile([P, SIGNALS * GROUP * NODES], BF16, tag="x_rows")
-            by_signal = x_rows[:].rearrange("c (x b n) -> c x b n", x=SIGNALS, b=GROUP)
+            by_signal = x_rows[:].rearrange("r (x f) -> r x f", x=SIGNALS)
             for x, signal in enumerate((inputs, state)):
                 nc.sync.dma_start(
                     out=by_signal[:, x],
-                    in_=signal[columns(g * GROUP, GROUP), :].rearrange("b (c n) -> c b n", n=NODES),
+                    in_=signal[columns(g * GROUP, GROUP), :].rearrange("b (q f) -> (b q) f", f=GROUP * NODES),
                 )
             return x_rows
 
@@ -93,13 +93,13 @@ def tile_gcrnncell_pa_t_kernel(tc, inputs, state, support0, support1, r_kernel, 
             else:
                 nc.scalar.copy(out=out, in_=in_)
 
-        def flip_two_blocks(engine, row_words, quad_words):
+        def flip_two_blocks(engine, row_words, quad_words, order):
             bank = psum.tile([P, BANK], F32, tag="bank")
             flipped = bank[:].rearrange("w (k u r) -> w k u r", k=2, u=HALVES)
             for k in range(2):
                 for u in range(HALVES):
                     nc.tensor.transpose(flipped[:, k, u, :], row_words[:, k, columns(u * P, P)], identity[:])
-            empty_bank(engine, quad_words, flipped.rearrange("w k u r -> w k r u"))
+            empty_bank(engine, quad_words, flipped.rearrange(order))
 
         def quantise(quads, operand, first_word, words):
             codes, scales = operand
@@ -133,7 +133,9 @@ def tile_gcrnncell_pa_t_kernel(tc, inputs, state, support0, support1, r_kernel, 
         def flip_supports(pair, engines):
             tiles = columns(2 * pair, 2)
             for i in range(SUPPORTS):
-                flip_two_blocks(engines[i], sup_row_words[:, i, tiles, :], sup_quad_words[:, i, tiles, :, :])
+                flip_two_blocks(
+                    engines[i], sup_row_words[:, i, tiles, :], sup_quad_words[:, i, tiles, :, :], "w k u r -> w k r u"
+                )
 
         def quantise_supports(pair):
             quantise(sup_quads, sup_mx, pair * sup_words // 2, sup_words // 2)
@@ -147,10 +149,9 @@ def tile_gcrnncell_pa_t_kernel(tc, inputs, state, support0, support1, r_kernel, 
             return x_quads, (x_codes, x_scales)
 
         def flip_signal(g, x, x_quads, engine):
-            row_words = x_rows_of[g][:].bitcast(F32).rearrange("c (k w) -> c k w", w=ROW_WORDS)
-            quad_words = x_quads[:].bitcast(F32).rearrange("w (k c u) -> w k c u", c=CHANNELS, u=HALVES)
-            blocks = columns(2 * x, 2)
-            flip_two_blocks(engine, row_words[:, blocks, :], quad_words[:, blocks, :, :])
+            row_words = x_rows_of[g][:].bitcast(F32).rearrange("r (x e w) -> r x e w", x=SIGNALS, w=ROW_WORDS)
+            quad_words = x_quads[:].bitcast(F32).rearrange("w (x r e u) -> w x r e u", x=SIGNALS, e=GROUP, u=HALVES)
+            flip_two_blocks(engine, row_words[:, x], quad_words[:, x], "w k u r -> w r k u")
 
         def quantise_signal(x, x_quads, x_mx):
             quantise(x_quads, x_mx, x * signal_words, signal_words)

@@ -46,6 +46,14 @@ def tile_gcrnncell_pa_t_kernel(tc, inputs, state, support0, support1, r_kernel, 
         gate_pool = stack.enter_context(tc.tile_pool(name="gate", bufs=8))
         psum = stack.enter_context(tc.psum_pool(name="psum", bufs=PSUM_BANKS))
 
+        zeros = const.tile([P, BANK], BF16)
+        nc.vector.memset(zeros[:], 0.0)
+
+        def keep_tensor_busy(times):
+            bank = psum.tile([P, BANK], F32, tag="bank")
+            for dummy in range(times):
+                nc.tensor.matmul(out=bank[:], lhsT=zeros[:, columns(0, P)], rhs=zeros[:], start=True, stop=True)
+
         sup_rows = const.tile([P, SUPPORTS * NODES * NODE_TILES], BF16)
         sup_rows_by_tile = sup_rows[:].rearrange("p (i t n) -> p i t n", i=SUPPORTS, t=NODE_TILES)
         supports = (support0, support1)
@@ -245,13 +253,27 @@ def tile_gcrnncell_pa_t_kernel(tc, inputs, state, support0, support1, r_kernel, 
             gate_values = start_gates()
             gates(hs_mx, gate_values, (0, 1))
             store_gates(b, gate_values, 0, NODE_TILES)
+        keep_tensor_busy(5)
+        gate_quads_by_gate = gate_quads[:].rearrange("c (g u j) -> c g u j", g=GATES, j=PACK)
+        for gate in range(GATES):
+            nc.gpsimd.tensor_scalar(
+                out=gate_quads_by_gate[:, gate],
+                in0=gate_rows_by_gate[:, gate].rearrange("c j u -> c u j"),
+                scalar1=1.0,
+                scalar2=0.0,
+                op0=mybir.AluOpType.mult,
+                op1=mybir.AluOpType.add,
+            )
 
         flip_supports(0, "SS")
+        keep_tensor_busy(1)
         quantise_supports(0)
         x_quads, x_mx = start_group()
         flip_signal(0, 0, x_quads, "S")
+        keep_tensor_busy(1)
         quantise_signal(0, x_quads, x_mx)
         flip_signal(0, 1, x_quads, "S")
+        keep_tensor_busy(1)
         quantise_signal(1, x_quads, x_mx)
         flip_supports(1, "SV")
         h_rows = start_h()
@@ -296,11 +318,6 @@ def tile_gcrnncell_pa_t_kernel(tc, inputs, state, support0, support1, r_kernel, 
             if turn == 0 and not last:
                 quantise_signal(0, next_quads, next_mx)
                 quantise_signal(1, next_quads, next_mx)
-            if b == 0:
-                nc.vector.tensor_copy(
-                    out=gate_quads[:].rearrange("c (g u j) -> c g u j", g=GATES, j=PACK),
-                    in_=gate_rows_by_gate.rearrange("c g j u -> c g u j"),
-                )
             if waiting:
                 all_gates(*waiting)
             waiting = (b, hs_mx)

@@ -138,9 +138,9 @@ def tile_gcrnncell_pa_t_kernel(tc, inputs, state, support0, support1, r_kernel, 
             "w (t i p u) -> w i t p u", t=NODE_TILES, i=SUPPORTS, u=HALVES
         )
 
-        def flip_supports(pair, engines):
+        def flip_supports(pair, engines, which=(0, 1)):
             tiles = columns(2 * pair, 2)
-            for i in range(SUPPORTS):
+            for i in which:
                 flip_two_blocks(
                     engines[i], sup_row_words[:, i, tiles, :], sup_quad_words[:, i, tiles, :, :], "w k u r -> w k r u"
                 )
@@ -208,10 +208,11 @@ def tile_gcrnncell_pa_t_kernel(tc, inputs, state, support0, support1, r_kernel, 
                     )
                 empty_bank(engine, by_tile[:, t], bank[:].rearrange("p (i b c) -> p i b c", i=SUPPORTS, b=GROUP))
 
-        def store_h(g, h_rows):
+        def store_h(g, h_rows, first_tile=0, tiles=NODE_TILES):
+            part = columns(first_tile * SUPPORTS * CHANNELS, tiles * SUPPORTS * CHANNELS)
             nc.sync.dma_start(
-                out=out_2[columns(g * GROUP, GROUP)].rearrange("b (p t) k -> p b (t k)", t=NODE_TILES),
-                in_=h_rows[:].rearrange("p (b r) -> p b r", b=GROUP),
+                out=out_2[columns(g * GROUP, GROUP)].rearrange("b (p t) k -> p b (t k)", t=NODE_TILES)[:, :, part],
+                in_=h_rows[:].rearrange("p (b r) -> p b r", b=GROUP)[:, :, part],
             )
 
         gate_words = GATES * CHANNELS
@@ -298,6 +299,8 @@ def tile_gcrnncell_pa_t_kernel(tc, inputs, state, support0, support1, r_kernel, 
                 if b == BATCH - 1:
                     diffuse_for_gates(b, x_mx, hs_quads, (0, 1), "VS")
                     quantise_hs(hs_quads, hs_mx, (0, 1))
+                    all_gates(*waiting)
+                    waiting = None
                     diffuse_for_gates(b, x_mx, hs_quads, (2, 3), "VS")
                     quantise_hs(hs_quads, hs_mx, (2, 3))
                 else:
@@ -306,8 +309,11 @@ def tile_gcrnncell_pa_t_kernel(tc, inputs, state, support0, support1, r_kernel, 
                 if turn == 0:
                     next_quads, next_mx = start_group()
                     flip_signal(g + 1, 0, next_quads, "S" if g == 0 else "V")
-                    flip_signal(g + 1, 1, next_quads, "SVS"[0 if g == 0 else 1 + g % 2])
+                    flip_signal(g + 1, 1, next_quads, "S" if g == 0 or g % 3 else "V")
                 else:
+                    if g == 6:
+                        all_gates(*waiting)
+                        waiting = None
                     if g == 0:
                         quantise(gate_quads, gate_mx, 0, gate_words)
                     h_rows = start_h()

@@ -129,9 +129,9 @@ def tile_gcrnncell_pa_t_kernel(tc, inputs, state, support0, support1, r_kernel, 
             )
 
         sup_words = NODE_TILES * SUPPORTS * P
-        sup_quads = const.tile([P, sup_words * PACK], BF16, align_bytes=64)
-        sup_codes = const.tile([P, sup_words], U32, align_bytes=64)
-        sup_scales = const.tile([P, sup_words], U8, align_bytes=64)
+        sup_quads = const.tile([P, sup_words * PACK], BF16, align_bytes=256)
+        sup_codes = const.tile([P, sup_words], U32, align_bytes=256)
+        sup_scales = const.tile([P, sup_words], U8, align_bytes=256)
         sup_mx = (sup_codes, sup_scales)
         sup_row_words = sup_rows[:].bitcast(F32).rearrange("p (i t w) -> p i t w", i=SUPPORTS, t=NODE_TILES)
         sup_quad_words = sup_quads[:].bitcast(F32).rearrange(
@@ -151,9 +151,9 @@ def tile_gcrnncell_pa_t_kernel(tc, inputs, state, support0, support1, r_kernel, 
         signal_words = GROUP * CHANNELS
 
         def start_group():
-            x_quads = group_pool.tile([P, SIGNALS * signal_words * PACK], BF16, tag="x_quads", align_bytes=64)
-            x_codes = group_pool.tile([P, SIGNALS * signal_words], U32, tag="x_codes", align_bytes=64)
-            x_scales = group_pool.tile([P, SIGNALS * signal_words], U8, tag="x_scales", align_bytes=64)
+            x_quads = group_pool.tile([P, SIGNALS * signal_words * PACK], BF16, tag="x_quads", align_bytes=256)
+            x_codes = group_pool.tile([P, SIGNALS * signal_words], U32, tag="x_codes", align_bytes=256)
+            x_scales = group_pool.tile([P, SIGNALS * signal_words], U8, tag="x_scales", align_bytes=256)
             return x_quads, (x_codes, x_scales)
 
         def flip_signal(g, x, x_quads, engine):
@@ -165,9 +165,9 @@ def tile_gcrnncell_pa_t_kernel(tc, inputs, state, support0, support1, r_kernel, 
             quantise(x_quads, x_mx, x * signal_words, signal_words)
 
         def start_hs():
-            hs_quads = batch_pool.tile([P, NODES * PACK], BF16, tag="hs_quads", align_bytes=64)
-            hs_codes = batch_pool.tile([P, NODES], U32, tag="hs_codes", align_bytes=64)
-            hs_scales = batch_pool.tile([P, NODES], U8, tag="hs_scales", align_bytes=64)
+            hs_quads = batch_pool.tile([P, NODES * PACK], BF16, tag="hs_quads", align_bytes=256)
+            hs_codes = batch_pool.tile([P, NODES], U32, tag="hs_codes", align_bytes=256)
+            hs_scales = batch_pool.tile([P, NODES], U8, tag="hs_scales", align_bytes=256)
             return hs_quads, (hs_codes, hs_scales)
 
         def diffuse_for_gates(b, x_mx, hs_quads, tiles, engines):
@@ -216,9 +216,9 @@ def tile_gcrnncell_pa_t_kernel(tc, inputs, state, support0, support1, r_kernel, 
             )
 
         gate_words = GATES * CHANNELS
-        gate_quads = const.tile([P, gate_words * PACK], BF16, align_bytes=64)
-        gate_codes = const.tile([P, gate_words], U32, align_bytes=64)
-        gate_scales = const.tile([P, gate_words], U8, align_bytes=64)
+        gate_quads = const.tile([P, gate_words * PACK], BF16, align_bytes=256)
+        gate_codes = const.tile([P, gate_words], U32, align_bytes=256)
+        gate_scales = const.tile([P, gate_words], U8, align_bytes=256)
         gate_mx = (gate_codes, gate_scales)
 
         def start_gates():

@@ -266,7 +266,9 @@ def tile_gcrnncell_pa_t_kernel(tc, inputs, state, support0, support1, r_kernel, 
                 op1=mybir.AluOpType.add,
             )
 
-        flip_supports(0, "SS")
+        flip_supports(0, "SS", (0,))
+        keep_tensor_busy(1)
+        flip_supports(0, "SS", (1,))
         keep_tensor_busy(1)
         quantise_supports(0)
         x_quads, x_mx = start_group()
@@ -276,7 +278,9 @@ def tile_gcrnncell_pa_t_kernel(tc, inputs, state, support0, support1, r_kernel, 
         flip_signal(0, 1, x_quads, "S")
         keep_tensor_busy(1)
         quantise_signal(1, x_quads, x_mx)
-        flip_supports(1, "SV")
+        flip_supports(1, "SV", (0,))
+        keep_tensor_busy(1)
+        flip_supports(1, "SV", (1,))
         h_rows = start_h()
         diffuse_for_output(0, x_mx, h_rows, (0, 1), "SS")
         quantise_supports(1)

from contextlib import ExitStack

import concourse.mybir as mybir
from concourse.masks import make_identity

F32 = mybir.dt.float32
BF16 = mybir.dt.bfloat16
U32 = mybir.dt.uint32
U8 = mybir.dt.uint8
FP8X4 = mybir.dt.float8_e4m3fn_x4
SIGMOID = mybir.ActivationFunctionType.Sigmoid

P = 128
PACK = 4
BANK = 512
PSUM_BANKS = 8

BATCH = 16
NODES = 512
CHANNELS = 128
SIGNALS = 2
SUPPORTS = 2
GATES = 2
NODE_TILES = NODES // P
ROW_WORDS = NODES // 2
HALVES = ROW_WORDS // P
GROUP = 2
GROUPS = BATCH // GROUP

FLOPS = 2 * BATCH * NODES * NODES * SUPPORTS * SIGNALS * CHANNELS + 2 * BATCH * NODES * (PACK * CHANNELS) * GATES * CHANNELS


def columns(first, count):
    return slice(first, first + count)


def tile_gcrnncell_pa_t_kernel(tc, inputs, state, support0, support1, r_kernel, u_kernel, out_0, out_1, out_2):
    nc = tc.nc
    with ExitStack() as stack:
        stack.enter_context(tc.manual_schedule())
        const = stack.enter_context(tc.tile_pool(name="const", bufs=1))
        rows_pool = stack.enter_context(tc.tile_pool(name="rows", bufs=GROUPS))
        group_pool = stack.enter_context(tc.tile_pool(name="group", bufs=3))
        batch_pool = stack.enter_context(tc.tile_pool(name="batch", bufs=3))
        h_pool = stack.enter_context(tc.tile_pool(name="h", bufs=4))
        gate_pool = stack.enter_context(tc.tile_pool(name="gate", bufs=8))
        psum = stack.enter_context(tc.psum_pool(name="psum", bufs=PSUM_BANKS))

        zeros = const.tile([P, BANK], BF16)
        nc.vector.memset(zeros[:], 0.0)

        def keep_tensor_busy(times):
            bank = psum.tile([P, BANK], F32, tag="bank")
            for dummy in range(times):
                nc.tensor.matmul(out=bank[:], lhsT=zeros[:, columns(0, P)], rhs=zeros[:], start=True, stop=True)

        sup_rows = const.tile([P, SUPPORTS * NODES * NODE_TILES], BF16)
        sup_rows_by_tile = sup_rows[:].rearrange("p (i t n) -> p i t n", i=SUPPORTS, t=NODE_TILES)
        supports = (support0, support1)

        def load_supports(pair):
            for i in range(SUPPORTS):
                tiles = columns(2 * pair, 2)
                nc.sync.dma_start(
                    out=sup_rows_by_tile[:, i, tiles, :],
                    in_=supports[i].rearrange("(p t) n -> p t n", t=NODE_TILES)[:, tiles, :],
                )

        def load_group(g):
            x_rows = rows_pool.tile([P, SIGNALS * GROUP * NODES], BF16, tag="x_rows")
            by_signal = x_rows[:].rearrange("r (x f) -> r x f", x=SIGNALS)
            for x, signal in enumerate((inputs, state)):
                nc.sync.dma_start(
                    out=by_signal[:, x],
                    in_=signal[columns(g * GROUP, GROUP), :].rearrange("b (q f) -> (b q) f", f=GROUP * NODES),
                )
            return x_rows

        x_rows_of = []
        load_supports(0)
        x_rows_of.append(load_group(0))
        load_supports(1)
        x_rows_of.append(load_group(1))

        gate_rows = const.tile([P, GATES * PACK * CHANNELS], BF16)
        gate_rows_by_gate = gate_rows[:].rearrange("c (g j u) -> c g j u", g=GATES, j=PACK)
        for gate, kernel in enumerate((r_kernel, u_kernel)):
            nc.sync.dma_start(out=gate_rows_by_gate[:, gate], in_=kernel.rearrange("(j c) u -> c j u", c=P))

        for g in range(2, GROUPS):
            x_rows_of.append(load_group(g))

        identity = const.tile([P, P], F32)
        make_identity(nc, identity[:])
        table_warmer = const.tile([P, 1], F32)
        nc.scalar.activation(out=table_warmer[:], in_=identity[:, 0:1], func=SIGMOID)

        def empty_bank(engine, out, in_):
            if engine == "V":
                nc.vector.tensor_copy(out=out, in_=in_)
            else:
                nc.scalar.copy(out=out, in_=in_)

        def flip_two_blocks(engine, row_words, quad_words, order):
            bank = psum.tile([P, BANK], F32, tag="bank")
            flipped = bank[:].rearrange("w (k u r) -> w k u r", k=2, u=HALVES)
            for k in range(2):
                for u in range(HALVES):
                    nc.tensor.transpose(flipped[:, k, u, :], row_words[:, k, columns(u * P, P)], identity[:])
            empty_bank(engine, quad_words, flipped.rearrange(order))

        def quantise(quads, operand, first_word, words):
            codes, scales = operand
            nc.vector.quantize_mx(
                out=codes[:, columns(first_word, words)].bitcast(FP8X4),
                scales=scales[:, columns(first_word, words)],
                in_=quads[:, columns(PACK * first_word, PACK * words)],
            )

        def multiply(out, stationary, stationary_columns, moving, moving_columns):
            nc.tensor.matmul_mx(
                out=out,
                lhsT=stationary[0][:, stationary_columns].bitcast(FP8X4),
                lhsT_scale=stationary[1][:, stationary_columns],
                rhs=moving[0][:, moving_columns].bitcast(FP8X4),
                rhs_scale=moving[1][:, moving_columns],
                start=True,
                stop=True,
            )

        sup_words = NODE_TILES * SUPPORTS * P
        sup_quads = const.tile([P, sup_words * PACK], BF16, align_bytes=256)
        sup_codes = const.tile([P, sup_words], U32, align_bytes=256)
        sup_scales = const.tile([P, sup_words], U8, align_bytes=256)
        sup_mx = (sup_codes, sup_scales)
        sup_row_words = sup_rows[:].bitcast(F32).rearrange("p (i t w) -> p i t w", i=SUPPORTS, t=NODE_TILES)
        sup_quad_words = sup_quads[:].bitcast(F32).rearrange(
            "w (t i p u) -> w i t p u", t=NODE_TILES, i=SUPPORTS, u=HALVES
        )

        def flip_supports(pair, engines, which=(0, 1)):
            tiles = columns(2 * pair, 2)
            for i in which:
                flip_two_blocks(
                    engines[i], sup_row_words[:, i, tiles, :], sup_quad_words[:, i, tiles, :, :], "w k u r -> w k r u"
                )

        def quantise_supports(pair):
            quantise(sup_quads, sup_mx, pair * sup_words // 2, sup_words // 2)

        signal_words = GROUP * CHANNELS

        def start_group():
            x_quads = group_pool.tile([P, SIGNALS * signal_words * PACK], BF16, tag="x_quads", align_bytes=256)
            x_codes = group_pool.tile([P, SIGNALS * signal_words], U32, tag="x_codes", align_bytes=256)
            x_scales = group_pool.tile([P, SIGNALS * signal_words], U8, tag="x_scales", align_bytes=256)
            return x_quads, (x_codes, x_scales)

        def flip_signal(g, x, x_quads, engine):
            row_words = x_rows_of[g][:].bitcast(F32).rearrange("r (x e w) -> r x e w", x=SIGNALS, w=ROW_WORDS)
            quad_words = x_quads[:].bitcast(F32).rearrange("w (x r e u) -> w x r e u", x=SIGNALS, e=GROUP, u=HALVES)
            flip_two_blocks(engine, row_words[:, x], quad_words[:, x], "w k u r -> w r k u")

        def quantise_signal(x, x_quads, x_mx):
            quantise(x_quads, x_mx, x * signal_words, signal_words)

        def start_hs():
            hs_quads = batch_pool.tile([P, NODES * PACK], BF16, tag="hs_quads", align_bytes=256)
            hs_codes = batch_pool.tile([P, NODES], U32, tag="hs_codes", align_bytes=256)
            hs_scales = batch_pool.tile([P, NODES], U8, tag="hs_scales", align_bytes=256)
            return hs_quads, (hs_codes, hs_scales)

        def diffuse_for_gates(b, x_mx, hs_quads, tiles, engines):
            for t, engine in zip(tiles, engines):
                bank = psum.tile([P, BANK], F32, tag="bank")
                for x in range(SIGNALS):
                    multiply(
                        bank[:, columns(x * SUPPORTS * P, SUPPORTS * P)],
                        x_mx,
                        columns((x * GROUP + b % GROUP) * CHANNELS, CHANNELS),
                        sup_mx,
                        columns(t * SUPPORTS * P, SUPPORTS * P),
                    )
                empty_bank(
                    engine,
                    hs_quads[:, columns(t * P * PACK, P * PACK)].rearrange("c (p j) -> c p j", j=PACK),
                    bank[:].rearrange("c (j p) -> c p j", j=PACK),
                )

        def quantise_hs(hs_quads, hs_mx, tiles):
            quantise(hs_quads, hs_mx, tiles[0] * P, len(tiles) * P)

        def start_h():
            h_rows = h_pool.tile([P, GROUP * NODE_TILES * SUPPORTS * CHANNELS], F32, tag="h_rows")
            return h_rows

        def diffuse_for_output(g, x_mx, h_rows, tiles, engines):
            by_tile = h_rows[:].rearrange("p (b t i c) -> p t i b c", b=GROUP, t=NODE_TILES, i=SUPPORTS)
            for t, engine in zip(tiles, engines):
                bank = psum.tile([P, BANK], F32, tag="bank")
                for i in range(SUPPORTS):
                    multiply(
                        bank[:, columns(i * signal_words, signal_words)],
                        sup_mx,
                        columns((t * SUPPORTS + i) * P, P),
                        x_mx,
                        columns(0, signal_words),
                    )
                empty_bank(engine, by_tile[:, t], bank[:].rearrange("p (i b c) -> p i b c", i=SUPPORTS, b=GROUP))

        def store_h(g, h_rows, first_tile=0, tiles=NODE_TILES):
            part = columns(first_tile * SUPPORTS * CHANNELS, tiles * SUPPORTS * CHANNELS)
            nc.sync.dma_start(
                out=out_2[columns(g * GROUP, GROUP)].rearrange("b (p t) k -> p b (t k)", t=NODE_TILES)[:, :, part],
                in_=h_rows[:].rearrange("p (b r) -> p b r", b=GROUP)[:, :, part],
            )

        gate_words = GATES * CHANNELS
        gate_quads = const.tile([P, gate_words * PACK], BF16, align_bytes=256)
        gate_codes = const.tile([P, gate_words], U32, align_bytes=256)
        gate_scales = const.tile([P, gate_words], U8, align_bytes=256)
        gate_mx = (gate_codes, gate_scales)

        def start_gates():
            gate_values = gate_pool.tile([P, GATES * NODE_TILES * CHANNELS], F32, tag="gate_values")
            return gate_values

        def gates(hs_mx, gate_values, pairs):
            by_tile = gate_values[:].rearrange("p (g t u) -> p t g u", g=GATES, t=NODE_TILES)
            for pair in pairs:
                bank = psum.tile([P, BANK], F32, tag="bank")
                for k in range(2):
                    multiply(
                        bank[:, columns(k * gate_words, gate_words)],
                        hs_mx,
                        columns((2 * pair + k) * P, P),
                        gate_mx,
                        columns(0, gate_words),
                    )
                nc.scalar.activation(
                    out=by_tile[:, columns(2 * pair, 2)],
                    in_=bank[:].rearrange("p (t g u) -> p t g u", t=2, g=GATES),
                    func=SIGMOID,
                )

        def store_gates(b, gate_values, first_tile, tiles):
            for gate, result in enumerate((out_0, out_1)):
                nc.sync.dma_start(
                    out=result[b].rearrange("(p t) u -> p (t u)", t=NODE_TILES)[:, columns(first_tile * CHANNELS, tiles * CHANNELS)],
                    in_=gate_values[:, columns((gate * NODE_TILES + first_tile) * CHANNELS, tiles * CHANNELS)],
                )

        def all_gates(b, hs_mx):
            gate_values = start_gates()
            gates(hs_mx, gate_values, (0, 1))
            store_gates(b, gate_values, 0, NODE_TILES)
        keep_tensor_busy(5)
        gate_quads_by_gate = gate_quads[:].rearrange("c (g u j) -> c g u j", g=GATES, j=PACK)
        for gate in range(GATES):
            nc.gpsimd.tensor_scalar(
                out=gate_quads_by_gate[:, gate],
                in0=gate_rows_by_gate[:, gate].rearrange("c j u -> c u j"),
                scalar1=1.0,
                scalar2=0.0,
                op0=mybir.AluOpType.mult,
                op1=mybir.AluOpType.add,
            )

        flip_supports(0, "SS", (0,))
        keep_tensor_busy(1)
        flip_supports(0, "SS", (1,))
        keep_tensor_busy(1)
        quantise_supports(0)
        x_quads, x_mx = start_group()
        flip_signal(0, 0, x_quads, "S")
        keep_tensor_busy(1)
        quantise_signal(0, x_quads, x_mx)
        flip_signal(0, 1, x_quads, "S")
        keep_tensor_busy(1)
        quantise_signal(1, x_quads, x_mx)
        flip_supports(1, "SV", (0,))
        keep_tensor_busy(1)
        flip_supports(1, "SV", (1,))
        h_rows = start_h()
        diffuse_for_output(0, x_mx, h_rows, (0, 1), "SS")
        quantise_supports(1)
        first_halves = []
        for b in range(GROUP):
            hs_quads, hs_mx = start_hs()
            diffuse_for_gates(b, x_mx, hs_quads, (0, 1), "SV")
            first_halves.append((hs_quads, hs_mx))
        diffuse_for_output(0, x_mx, h_rows, (2, 3), "SV")
        store_h(0, h_rows)
        waiting = None
        for b in range(BATCH):
            g, turn = divmod(b, GROUP)
            last = g + 1 == GROUPS
            if b < GROUP:
                hs_quads, hs_mx = first_halves[b]
                diffuse_for_gates(b, x_mx, hs_quads, (2, 3), "SV")
            else:
                hs_quads, hs_mx = start_hs()
                if b == BATCH - 1:
                    diffuse_for_gates(b, x_mx, hs_quads, (0, 1), "VS")
                    quantise_hs(hs_quads, hs_mx, (0, 1))
                    all_gates(*waiting)
                    waiting = None
                    diffuse_for_gates(b, x_mx, hs_quads, (2, 3), "VS")
                    quantise_hs(hs_quads, hs_mx, (2, 3))
                else:
                    diffuse_for_gates(b, x_mx, hs_quads, (0, 1, 2, 3), "SVSV")
            if not last:
                if turn == 0:
                    next_quads, next_mx = start_group()
                    flip_signal(g + 1, 0, next_quads, "S" if g == 0 else "V")
                    flip_signal(g + 1, 1, next_quads, "S" if g == 0 or g % 3 else "V")
                else:
                    if g == 6:
                        all_gates(*waiting)
                        waiting = None
                    if g == 0:
                        quantise(gate_quads, gate_mx, 0, gate_words)
                    h_rows = start_h()
                    diffuse_for_output(g + 1, next_mx, h_rows, (0, 1, 2, 3), "SVSV")
                    store_h(g + 1, h_rows)
            if b < BATCH - 1:
                quantise_hs(hs_quads, hs_mx, (0, 1, 2, 3))
            if turn == 0 and not last:
                quantise_signal(0, next_quads, next_mx)
                quantise_signal(1, next_quads, next_mx)
            if waiting:
                all_gates(*waiting)
            waiting = (b, hs_mx)
            if turn == 1 and not last:
                x_mx = next_mx
        gate_values = start_gates()
        for pair in range(2):
            gates(hs_mx, gate_values, (pair,))
            store_gates(BATCH - 1, gate_values, 2 * pair, 2)
